import numpy as np
import ml_dtypes


def mxq(x, axis, fmt="e4m3"):
    dtype, down = {"e4m3": (ml_dtypes.float8_e4m3fn, 7), "e5m2": (ml_dtypes.float8_e5m2, 14)}[fmt]
    v = np.moveaxis(np.asarray(x, np.float32).astype(ml_dtypes.bfloat16).astype(np.float64), axis, -1)
    blocks = v.reshape(v.shape[:-1] + (-1, 32))
    amax = np.abs(blocks).max(-1, keepdims=True)
    byte = np.maximum(np.where(amax > 0, np.frexp(amax)[1] - 1 + 127, 0) - down, 1)
    scale = np.exp2(byte - 127.0)
    codes = (blocks / scale).astype(np.float32).astype(dtype).astype(np.float64)
    return np.moveaxis((codes * scale).reshape(v.shape), -1, axis)


WIDE = False


def mx_kscale(k):
    if not WIDE:
        return np.ones(k)
    levels = np.array([10, -10, 5, -5, 0])
    a = np.random.permutation(np.resize(levels, k // 512 * 4)).reshape(k // 512, 4)
    idx = np.arange(k)
    return np.exp2(a[idx // 512, idx % 128 // 32])


BF16 = ml_dtypes.bfloat16


def bf(x):
    return np.asarray(x, np.float32).astype(BF16)


def f64(x):
    return np.asarray(x).astype(np.float64)


E2M1 = np.array([0.0, 0.5, 1.0, 1.5, 2.0, 3.0, 4.0, 6.0, -0.0, -0.5, -1.0, -1.5, -2.0, -3.0, -4.0, -6.0])


def pack_weight(w, fmt):
    k, n = w.shape
    w = f64(bf(w)).reshape(k // 32, 32, n)
    amax = np.abs(w).max(1)
    if fmt == "e4m3":
        byte = np.frexp(amax)[1] - 1 + 127 - 7
    else:
        mant, ex = np.frexp(amax / 6.0)
        byte = np.where(mant > 0.5, ex, ex - 1) + 127
    byte = np.clip(np.where(amax > 0, byte, 1), 1, 254)
    scaled = (w * np.exp2(127.0 - byte)[:, None, :]).reshape(k, n).astype(np.float32)
    by_word = np.ascontiguousarray(scaled.reshape(k // 512, 128, 4, n).transpose(0, 1, 3, 2))
    if fmt == "e4m3":
        words = by_word.astype(ml_dtypes.float8_e4m3fn).view(np.uint8)
    else:
        c = by_word.astype(ml_dtypes.float4_e2m1fn).view(np.uint8) & 0xF
        words = c[..., 0::2] | (c[..., 1::2] << 4)
    return np.ascontiguousarray(words), np.ascontiguousarray(byte.astype(np.uint8).reshape(k // 512, 16, n))


def unpack_weight(words, scales, fmt):
    g, p, n, _ = words.shape
    if fmt == "e4m3":
        vals = np.ascontiguousarray(words).view(ml_dtypes.float8_e4m3fn).astype(np.float64)
    else:
        nib = np.empty((g, p, n, 4), np.uint8)
        nib[..., 0::2] = words & 0xF
        nib[..., 1::2] = words >> 4
        vals = E2M1[nib]
    vals = vals * np.repeat(np.exp2(scales.astype(np.float64) - 127.0), 8, axis=1)[..., None]
    return vals.transpose(0, 1, 3, 2).reshape(g * 512, n)


B, S, H, I, G = 2, 256, 1024, 2048, 4
T = B * S
FMT = "e4m3"


def grouped_linear(xf, words, scales, b, din, dout):
    w = unpack_weight(words, scales, FMT).reshape(G, din, dout)
    xg = xf.reshape(G, -1, din)
    y = (mxq(xg, 2, "e4m3") @ w) + b[:, None, :]
    return y.reshape(-1, dout)


def setup_inputs():
    s, t = mx_kscale(H), mx_kscale(I)
    hf = bf(np.random.standard_normal((T, H)) * s)
    g1 = np.random.standard_normal((G, I, H)) / np.sqrt(H) / s[None, None, :] * t[None, :, None]
    g1_b = bf(np.random.standard_normal((G, I)) * 0.3 * t[None, :])
    g2 = np.random.standard_normal((G, H, I)) / np.sqrt(I) / t[None, None, :]
    g2_b = bf(np.random.standard_normal((G, H)) * 0.3)
    g1_words, g1_scales = pack_weight(np.ascontiguousarray(g1.swapaxes(1, 2)).reshape(-1, I), FMT)
    g2_words, g2_scales = pack_weight(np.ascontiguousarray(g2.swapaxes(1, 2)).reshape(-1, H), FMT)
    return {"hf": hf,
            "g1_w_words": g1_words,
            "g1_w_scales": g1_scales,
            "g1_b": g1_b,
            "g2_w_words": g2_words,
            "g2_w_scales": g2_scales,
            "g2_b": g2_b}


def reference(hf, g1_w_words, g1_w_scales, g1_b, g2_w_words, g2_w_scales, g2_b):
    y = grouped_linear(f64(hf), g1_w_words, g1_w_scales, f64(g1_b), H, I)
    return grouped_linear(y, g2_w_words, g2_w_scales, f64(g2_b), I, H)

@@ -1,0 +1,193 @@
+from contextlib import ExitStack
+
+import concourse.mybir as mybir
+from concourse.masks import make_identity
+
+F32 = mybir.dt.float32
+BF16 = mybir.dt.bfloat16
+I32 = mybir.dt.int32
+U32 = mybir.dt.uint32
+U8 = mybir.dt.uint8
+FP8X4 = mybir.dt.float8_e4m3fn_x4
+ADD = mybir.AluOpType.add
+
+P = 128
+PACK = 4
+K_PASS = P * PACK
+GROUPS = 4
+HIDDEN = 1024
+INNER = 2048
+N_TILE = 512
+PASSES_1 = HIDDEN // K_PASS
+PASSES_2 = INNER // K_PASS
+QUADS = 4
+SHARED = 4
+
+FLOPS = 2 * GROUPS * P * HIDDEN * INNER * 2
+
+
+def load_words(nc, words_tile, words):
+    nc.sync.dma_start(
+        out=words_tile[:].bitcast(I32),
+        in_=words.rearrange("p n t -> p (n t)").bitcast(I32),
+    )
+
+
+def load_planes(nc, planes, scales):
+    for quad in range(QUADS):
+        nc.sync.dma_start(
+            out=planes[32 * quad : 32 * quad + 4 * SHARED, :].bitcast(I32),
+            in_=scales[:, 4 * quad : 4 * quad + 4, :].bitcast(I32),
+        )
+
+
+def tile_dummytemodel_pa_e_kernel(
+    tc, hf, g1_w_words, g1_w_scales, g1_b, g2_w_words, g2_w_scales, g2_b, out
+):
+    nc = tc.nc
+    with ExitStack() as ctx:
+        keep = ctx.enter_context(tc.tile_pool(name="keep", bufs=1))
+        work = ctx.enter_context(tc.tile_pool(name="work", bufs=2))
+        results = ctx.enter_context(tc.tile_pool(name="results", bufs=GROUPS * HIDDEN // N_TILE))
+        sums = ctx.enter_context(tc.psum_pool(name="sums", bufs=4))
+        turned = ctx.enter_context(tc.psum_pool(name="turned", bufs=4))
+        ctx.enter_context(tc.manual_schedule())
+
+        hf_rows = keep.tile([P, GROUPS, HIDDEN], BF16)
+        w1 = [keep.tile([P, INNER], U32, name="w1_%d" % g, align_bytes=64) for g in range(GROUPS * PASSES_1)]
+        w2 = [keep.tile([P, HIDDEN], U32, name="w2_%d" % g, align_bytes=64) for g in range(GROUPS * PASSES_2)]
+        w1_planes = [
+            keep.tile([P, INNER], U8, name="w1_planes_%d" % s, align_bytes=64)
+            for s in range(GROUPS * PASSES_1 // SHARED)
+        ]
+        w2_planes = [
+            keep.tile([P, HIDDEN], U8, name="w2_planes_%d" % s, align_bytes=64)
+            for s in range(GROUPS * PASSES_2 // SHARED)
+        ]
+        b1_rows = keep.tile([P, K_PASS], BF16)
+        b2_rows = keep.tile([P, HIDDEN], BF16)
+        ident_f32 = keep.tile([P, P], F32)
+        ident_bf16 = keep.tile([P, P], BF16)
+
+        nc.vector.memset(w1_planes[0][:].bitcast(I32), 0)
+        nc.vector.memset(b1_rows[:], 0.0)
+        nc.vector.memset(b2_rows[:], 0.0)
+        nc.vector.memset(w1_planes[1][:].bitcast(I32), 0)
+        for planes in w2_planes:
+            nc.vector.memset(planes[:].bitcast(I32), 0)
+        make_identity(nc, ident_f32[:])
+        make_identity(nc, ident_bf16[:])
+
+        nc.sync.dma_start(out=hf_rows[:], in_=hf.rearrange("(e p) k -> p e k", p=P))
+        nc.scalar.dma_start(out=b1_rows[0 : GROUPS * PASSES_2, :], in_=g1_b.rearrange("e (j c) -> (e j) c", c=K_PASS))
+        nc.scalar.dma_start(out=b2_rows[0:GROUPS, :], in_=g2_b)
+        for s in range(len(w1_planes)):
+            load_words(nc, w1[SHARED * s], g1_w_words[SHARED * s])
+            load_planes(nc, w1_planes[s], g1_w_scales[SHARED * s : SHARED * (s + 1)])
+            for g in range(SHARED * s + 1, SHARED * (s + 1)):
+                load_words(nc, w1[g], g1_w_words[g])
+        for s in range(len(w2_planes)):
+            load_planes(nc, w2_planes[s], g2_w_scales[SHARED * s : SHARED * (s + 1)])
+            for g in range(SHARED * s, SHARED * (s + 1)):
+                load_words(nc, w2[g], g2_w_words[g])
+
+        hf_grouped = keep.tile([P, GROUPS, PASSES_1 * P * 2], F32, align_bytes=64)
+        hf_codes = keep.tile([P, GROUPS, PASSES_1 * P], U32, align_bytes=64)
+        hf_scales = keep.tile([P, GROUPS, PASSES_1 * P], U8, align_bytes=64)
+        for e in range(GROUPS):
+            hf_words = hf_rows[:, e, :].bitcast(F32)
+            hf_t = turned.tile([P, PASSES_1, 2, P], F32, tag="turned")
+            for c in range(PASSES_1):
+                for u in range(2):
+                    nc.tensor.transpose(
+                        out=hf_t[:, c, u, :],
+                        in_=hf_words[:, 256 * c + u : 256 * (c + 1) : 2],
+                        identity=ident_f32[:],
+                    )
+            nc.scalar.copy(
+                out=hf_grouped[:, e, :].rearrange("p (c r u) -> p c r u", c=PASSES_1, u=2),
+                in_=hf_t[:].rearrange("p c u r -> p c r u"),
+            )
+            nc.vector.quantize_mx(
+                out=hf_codes[:, e, :].bitcast(FP8X4),
+                scales=hf_scales[:, e, :],
+                in_=hf_grouped[:, e, :].bitcast(BF16),
+            )
+
+        b1_t_psum = turned.tile([P, PACK, P], BF16, tag="turned")
+        for t in range(PACK):
+            nc.tensor.transpose(out=b1_t_psum[:, t, :], in_=b1_rows[:, t:K_PASS:PACK], identity=ident_bf16[:])
+        b1_t = keep.tile([P, GROUPS * PASSES_2, PACK], F32)
+        nc.vector.tensor_copy(
+            out=b1_t[:], in_=b1_t_psum[:, :, 0 : GROUPS * PASSES_2].rearrange("p t q -> p q t")
+        )
+
+        y_codes = [keep.tile([P, PASSES_2 * P], U32, name="y_codes_%d" % e, align_bytes=64) for e in range(GROUPS)]
+        y_scales = [keep.tile([P, PASSES_2 * P], U8, name="y_scales_%d" % e, align_bytes=64) for e in range(GROUPS)]
+        for e in range(GROUPS):
+            y_sums = [sums.tile([P, N_TILE], F32, name="y_sum_%d" % j, tag="sum") for j in range(PASSES_2)]
+            for c in range(PASSES_1):
+                g = PASSES_1 * e + c
+                for j in range(PASSES_2):
+                    cols = slice(N_TILE * j, N_TILE * (j + 1))
+                    nc.tensor.matmul_mx(
+                        out=y_sums[j][:],
+                        lhsT=hf_codes[:, e, P * c : P * (c + 1)].bitcast(FP8X4),
+                        lhsT_scale=hf_scales[:, e, P * c : P * (c + 1)],
+                        rhs=w1[g][:, cols].bitcast(FP8X4),
+                        rhs_scale=w1_planes[g // SHARED][4 * (g % SHARED) : P, cols],
+                        start=(c == 0),
+                        stop=(c == PASSES_1 - 1),
+                    )
+            y_rows = work.tile([P, PASSES_2, PACK, P], F32)
+            for j in range(PASSES_2):
+                nc.scalar.copy(out=y_rows[:, j, :, :], in_=y_sums[j][:].rearrange("r (p t) -> r t p", t=PACK))
+            y_grouped = work.tile([P, PASSES_2, P, PACK], BF16, align_bytes=64)
+            for j in range(PASSES_2):
+                y_t = turned.tile([P, PACK, P], F32, tag="turned")
+                for t in range(PACK):
+                    nc.tensor.transpose(out=y_t[:, t, :], in_=y_rows[:, j, t, :], identity=ident_f32[:])
+                nc.vector.tensor_tensor(
+                    out=y_grouped[:, j, :, :],
+                    in0=y_t[:].rearrange("p t r -> p r t"),
+                    in1=b1_t[:, PASSES_2 * e + j, :].unsqueeze(1).to_broadcast([P, P, PACK]),
+                    op=ADD,
+                )
+            nc.vector.quantize_mx(
+                out=y_codes[e][:].bitcast(FP8X4),
+                scales=y_scales[e][:],
+                in_=y_grouped[:].rearrange("p j r t -> p (j r t)"),
+            )
+
+        for e in range(GROUPS):
+            b2_all = work.tile([P, HIDDEN], F32)
+            for h in range(HIDDEN // N_TILE):
+                cols = slice(N_TILE * h, N_TILE * (h + 1))
+                b2_sum = sums.tile([P, N_TILE], F32, tag="sum")
+                nc.tensor.matmul(
+                    out=b2_sum[:],
+                    lhsT=ident_bf16[:, e : e + 1].to_broadcast([P, P]),
+                    rhs=b2_rows[:, cols],
+                    start=True,
+                    stop=True,
+                )
+                nc.scalar.copy(out=b2_all[:, cols], in_=b2_sum[:])
+            out_sums = [sums.tile([P, N_TILE], F32, name="out_sum_%d" % h, tag="sum") for h in range(HIDDEN // N_TILE)]
+            for j in range(PASSES_2):
+                g = PASSES_2 * e + j
+                for h in range(HIDDEN // N_TILE):
+                    cols = slice(N_TILE * h, N_TILE * (h + 1))
+                    nc.tensor.matmul_mx(
+                        out=out_sums[h][:],
+                        lhsT=y_codes[e][:, P * j : P * (j + 1)].bitcast(FP8X4),
+                        lhsT_scale=y_scales[e][:, P * j : P * (j + 1)],
+                        rhs=w2[g][:, cols].bitcast(FP8X4),
+                        rhs_scale=w2_planes[g // SHARED][4 * (g % SHARED) : P, cols],
+                        start=(j == 0),
+                        stop=(j == PASSES_2 - 1),
+                    )
+            for h in range(HIDDEN // N_TILE):
+                cols = slice(N_TILE * h, N_TILE * (h + 1))
+                result = results.tile([P, N_TILE], F32)
+                nc.vector.tensor_tensor(out=result[:], in0=out_sums[h][:], in1=b2_all[:, cols], op=ADD)
+                nc.sync.dma_start(out=out[P * e : P * (e + 1), cols], in_=result[:])

@@ -35,9 +35,9 @@ def load_words(nc, words_tile, words):
 
 def load_planes(nc, planes, scales):
     for quad in range(QUADS):
-        nc.sync.dma_start(
-            out=planes[32 * quad : 32 * quad + 4 * SHARED, :].bitcast(I32),
-            in_=scales[:, 4 * quad : 4 * quad + 4, :].bitcast(I32),
+        nc.gpsimd.dma_start(
+            out=planes[32 * quad : 32 * quad + 4 * SHARED, :].bitcast(F32),
+            in_=scales[:, 4 * quad : 4 * quad + 4, :].bitcast(F32),
         )
 
 

@@ -22,6 +22,8 @@ PASSES_1 = HIDDEN // K_PASS
 PASSES_2 = INNER // K_PASS
 QUADS = 4
 SHARED = 4
+BLOCKS = 2
+UNITS = GROUPS * PASSES_2 // BLOCKS
 
 FLOPS = 2 * GROUPS * P * HIDDEN * INNER * 2
 
@@ -114,24 +116,21 @@ def tile_dummytemodel_pa_e_kernel(
                 in_=hf_grouped[:, e, :].bitcast(BF16),
             )
 
-        b1_t_psum = turned.tile([P, PACK, P], BF16, tag="turned")
-        for t in range(PACK):
-            nc.tensor.transpose(out=b1_t_psum[:, t, :], in_=b1_rows[:, t:K_PASS:PACK], identity=ident_bf16[:])
-        b1_t = keep.tile([P, GROUPS * PASSES_2, PACK], F32)
-        nc.vector.tensor_copy(
-            out=b1_t[:], in_=b1_t_psum[:, :, 0 : GROUPS * PASSES_2].rearrange("p t q -> p q t")
-        )
-
         y_codes = [keep.tile([P, PASSES_2 * P], U32, name="y_codes_%d" % e, align_bytes=64) for e in range(GROUPS)]
         y_scales = [keep.tile([P, PASSES_2 * P], U8, name="y_scales_%d" % e, align_bytes=64) for e in range(GROUPS)]
-        for e in range(GROUPS):
-            y_sums = [sums.tile([P, N_TILE], F32, name="y_sum_%d" % j, tag="sum") for j in range(PASSES_2)]
-            for c in range(PASSES_1):
-                g = PASSES_1 * e + c
-                for j in range(PASSES_2):
-                    cols = slice(N_TILE * j, N_TILE * (j + 1))
+        b1_t = keep.tile([P, GROUPS * PASSES_2, PACK], F32)
+
+        def multiply(unit):
+            first_block = BLOCKS * unit
+            y_rows = work.tile([P, BLOCKS, PACK, P], F32)
+            for b in range(BLOCKS):
+                e, j = divmod(first_block + b, PASSES_2)
+                cols = slice(N_TILE * j, N_TILE * (j + 1))
+                y_sum = sums.tile([P, N_TILE], F32, tag="sum")
+                for c in range(PASSES_1):
+                    g = PASSES_1 * e + c
                     nc.tensor.matmul_mx(
-                        out=y_sums[j][:],
+                        out=y_sum[:],
                         lhsT=hf_codes[:, e, P * c : P * (c + 1)].bitcast(FP8X4),
                         lhsT_scale=hf_scales[:, e, P * c : P * (c + 1)],
                         rhs=w1[g][:, cols].bitcast(FP8X4),
@@ -139,25 +138,43 @@ def tile_dummytemodel_pa_e_kernel(
                         start=(c == 0),
                         stop=(c == PASSES_1 - 1),
                     )
-            y_rows = work.tile([P, PASSES_2, PACK, P], F32)
-            for j in range(PASSES_2):
-                nc.scalar.copy(out=y_rows[:, j, :, :], in_=y_sums[j][:].rearrange("r (p t) -> r t p", t=PACK))
-            y_grouped = work.tile([P, PASSES_2, P, PACK], BF16, align_bytes=64)
-            for j in range(PASSES_2):
+                nc.scalar.copy(out=y_rows[:, b, :, :], in_=y_sum[:].rearrange("r (p t) -> r t p", t=PACK))
+            return y_rows
+
+        def turn_and_quantise(unit, y_rows):
+            first_block = BLOCKS * unit
+            y_grouped = work.tile([P, BLOCKS, P, PACK], BF16, align_bytes=64)
+            for b in range(BLOCKS):
                 y_t = turned.tile([P, PACK, P], F32, tag="turned")
                 for t in range(PACK):
-                    nc.tensor.transpose(out=y_t[:, t, :], in_=y_rows[:, j, t, :], identity=ident_f32[:])
+                    nc.tensor.transpose(out=y_t[:, t, :], in_=y_rows[:, b, t, :], identity=ident_f32[:])
                 nc.vector.tensor_tensor(
-                    out=y_grouped[:, j, :, :],
+                    out=y_grouped[:, b, :, :],
                     in0=y_t[:].rearrange("p t r -> p r t"),
-                    in1=b1_t[:, PASSES_2 * e + j, :].unsqueeze(1).to_broadcast([P, P, PACK]),
+                    in1=b1_t[:, first_block + b, :].unsqueeze(1).to_broadcast([P, P, PACK]),
                     op=ADD,
                 )
+            e, j = divmod(first_block, PASSES_2)
             nc.vector.quantize_mx(
-                out=y_codes[e][:].bitcast(FP8X4),
-                scales=y_scales[e][:],
-                in_=y_grouped[:].rearrange("p j r t -> p (j r t)"),
+                out=y_codes[e][:, P * j : P * (j + BLOCKS)].bitcast(FP8X4),
+                scales=y_scales[e][:, P * j : P * (j + BLOCKS)],
+                in_=y_grouped[:].rearrange("p b r t -> p (b r t)"),
             )
+
+        waiting = multiply(0)
+
+        b1_t_psum = turned.tile([P, PACK, P], BF16, tag="turned")
+        for t in range(PACK):
+            nc.tensor.transpose(out=b1_t_psum[:, t, :], in_=b1_rows[:, t:K_PASS:PACK], identity=ident_bf16[:])
+        nc.vector.tensor_copy(
+            out=b1_t[:], in_=b1_t_psum[:, :, 0 : GROUPS * PASSES_2].rearrange("p t q -> p q t")
+        )
+
+        for unit in range(1, UNITS):
+            fresh = multiply(unit)
+            turn_and_quantise(unit - 1, waiting)
+            waiting = fresh
+        turn_and_quantise(UNITS - 1, waiting)
 
         for e in range(GROUPS):
             b2_all = work.tile([P, HIDDEN], F32)

@@ -116,6 +116,23 @@ def tile_dummytemodel_pa_e_kernel(
                 in_=hf_grouped[:, e, :].bitcast(BF16),
             )
 
+        b2_all = keep.tile([P, GROUPS, HIDDEN], F32)
+        for e in range(GROUPS):
+            for h in range(HIDDEN // N_TILE):
+                cols = slice(N_TILE * h, N_TILE * (h + 1))
+                b2_sum = sums.tile([P, N_TILE], F32, tag="sum")
+                nc.tensor.matmul(
+                    out=b2_sum[:],
+                    lhsT=ident_bf16[:, e : e + 1].to_broadcast([P, P]),
+                    rhs=b2_rows[:, cols],
+                    start=True,
+                    stop=True,
+                )
+                if h == 0:
+                    nc.scalar.copy(out=b2_all[:, e, cols], in_=b2_sum[:])
+                else:
+                    nc.vector.tensor_copy(out=b2_all[:, e, cols], in_=b2_sum[:])
+
         y_codes = [keep.tile([P, PASSES_2 * P], U32, name="y_codes_%d" % e, align_bytes=64) for e in range(GROUPS)]
         y_scales = [keep.tile([P, PASSES_2 * P], U8, name="y_scales_%d" % e, align_bytes=64) for e in range(GROUPS)]
         b1_t = keep.tile([P, GROUPS * PASSES_2, PACK], F32)
@@ -177,18 +194,6 @@ def tile_dummytemodel_pa_e_kernel(
         turn_and_quantise(UNITS - 1, waiting)
 
         for e in range(GROUPS):
-            b2_all = work.tile([P, HIDDEN], F32)
-            for h in range(HIDDEN // N_TILE):
-                cols = slice(N_TILE * h, N_TILE * (h + 1))
-                b2_sum = sums.tile([P, N_TILE], F32, tag="sum")
-                nc.tensor.matmul(
-                    out=b2_sum[:],
-                    lhsT=ident_bf16[:, e : e + 1].to_broadcast([P, P]),
-                    rhs=b2_rows[:, cols],
-                    start=True,
-                    stop=True,
-                )
-                nc.scalar.copy(out=b2_all[:, cols], in_=b2_sum[:])
             out_sums = [sums.tile([P, N_TILE], F32, name="out_sum_%d" % h, tag="sum") for h in range(HIDDEN // N_TILE)]
             for j in range(PASSES_2):
                 g = PASSES_2 * e + j
@@ -206,5 +211,5 @@ def tile_dummytemodel_pa_e_kernel(
             for h in range(HIDDEN // N_TILE):
                 cols = slice(N_TILE * h, N_TILE * (h + 1))
                 result = results.tile([P, N_TILE], F32)
-                nc.vector.tensor_tensor(out=result[:], in0=out_sums[h][:], in1=b2_all[:, cols], op=ADD)
+                nc.vector.tensor_tensor(out=result[:], in0=out_sums[h][:], in1=b2_all[:, e, cols], op=ADD)
                 nc.sync.dma_start(out=out[P * e : P * (e + 1), cols], in_=result[:])

@@ -55,7 +55,8 @@ def tile_dummytemodel_pa_e_kernel(
         turned = ctx.enter_context(tc.psum_pool(name="turned", bufs=4))
         ctx.enter_context(tc.manual_schedule())
 
-        hf_rows = keep.tile([P, GROUPS, HIDDEN], BF16)
+        b1_t = keep.tile([P, GROUPS * PASSES_2 + 4, PACK], F32, align_bytes=256)
+        hf_rows = keep.tile([P, GROUPS, HIDDEN], BF16, align_bytes=64)
         w1 = [keep.tile([P, INNER], U32, name="w1_%d" % g, align_bytes=64) for g in range(GROUPS * PASSES_1)]
         w2 = [keep.tile([P, HIDDEN], U32, name="w2_%d" % g, align_bytes=64) for g in range(GROUPS * PASSES_2)]
         w1_planes = [
@@ -135,7 +136,6 @@ def tile_dummytemodel_pa_e_kernel(
 
         y_codes = [keep.tile([P, PASSES_2 * P], U32, name="y_codes_%d" % e, align_bytes=64) for e in range(GROUPS)]
         y_scales = [keep.tile([P, PASSES_2 * P], U8, name="y_scales_%d" % e, align_bytes=64) for e in range(GROUPS)]
-        b1_t = keep.tile([P, GROUPS * PASSES_2, PACK], F32)
 
         def multiply(unit):
             first_block = BLOCKS * unit
@@ -184,7 +184,7 @@ def tile_dummytemodel_pa_e_kernel(
         for t in range(PACK):
             nc.tensor.transpose(out=b1_t_psum[:, t, :], in_=b1_rows[:, t:K_PASS:PACK], identity=ident_bf16[:])
         nc.vector.tensor_copy(
-            out=b1_t[:], in_=b1_t_psum[:, :, 0 : GROUPS * PASSES_2].rearrange("p t q -> p q t")
+            out=b1_t[:, 0 : GROUPS * PASSES_2, :], in_=b1_t_psum[:, :, 0 : GROUPS * PASSES_2].rearrange("p t q -> p q t")
         )
 
         for unit in range(1, UNITS):

@@ -55,10 +55,10 @@ def tile_dummytemodel_pa_e_kernel(
         turned = ctx.enter_context(tc.psum_pool(name="turned", bufs=4))
         ctx.enter_context(tc.manual_schedule())
 
+        w1 = [keep.tile([P, INNER], U32, name="w1_%d" % g, align_bytes=256) for g in range(GROUPS * PASSES_1)]
+        w2 = [keep.tile([P, HIDDEN], U32, name="w2_%d" % g, align_bytes=256) for g in range(GROUPS * PASSES_2)]
         b1_t = keep.tile([P, GROUPS * PASSES_2 + 4, PACK], F32, align_bytes=256)
         hf_rows = keep.tile([P, GROUPS, HIDDEN], BF16, align_bytes=64)
-        w1 = [keep.tile([P, INNER], U32, name="w1_%d" % g, align_bytes=64) for g in range(GROUPS * PASSES_1)]
-        w2 = [keep.tile([P, HIDDEN], U32, name="w2_%d" % g, align_bytes=64) for g in range(GROUPS * PASSES_2)]
         w1_planes = [
             keep.tile([P, INNER], U8, name="w1_planes_%d" % s, align_bytes=64)
             for s in range(GROUPS * PASSES_1 // SHARED)

from contextlib import ExitStack

import concourse.mybir as mybir
from concourse.masks import make_identity

F32 = mybir.dt.float32
BF16 = mybir.dt.bfloat16
I32 = mybir.dt.int32
U32 = mybir.dt.uint32
U8 = mybir.dt.uint8
FP8X4 = mybir.dt.float8_e4m3fn_x4
ADD = mybir.AluOpType.add

P = 128
PACK = 4
K_PASS = P * PACK
GROUPS = 4
HIDDEN = 1024
INNER = 2048
N_TILE = 512
PASSES_1 = HIDDEN // K_PASS
PASSES_2 = INNER // K_PASS
QUADS = 4
SHARED = 4
BLOCKS = 2
UNITS = GROUPS * PASSES_2 // BLOCKS

FLOPS = 2 * GROUPS * P * HIDDEN * INNER * 2


def load_words(nc, words_tile, words):
    nc.sync.dma_start(
        out=words_tile[:].bitcast(I32),
        in_=words.rearrange("p n t -> p (n t)").bitcast(I32),
    )


def load_planes(nc, planes, scales):
    for quad in range(QUADS):
        nc.gpsimd.dma_start(
            out=planes[32 * quad : 32 * quad + 4 * SHARED, :].bitcast(F32),
            in_=scales[:, 4 * quad : 4 * quad + 4, :].bitcast(F32),
        )


def tile_dummytemodel_pa_e_kernel(
    tc, hf, g1_w_words, g1_w_scales, g1_b, g2_w_words, g2_w_scales, g2_b, out
):
    nc = tc.nc
    with ExitStack() as ctx:
        keep = ctx.enter_context(tc.tile_pool(name="keep", bufs=1))
        work = ctx.enter_context(tc.tile_pool(name="work", bufs=2))
        results = ctx.enter_context(tc.tile_pool(name="results", bufs=GROUPS * HIDDEN // N_TILE))
        sums = ctx.enter_context(tc.psum_pool(name="sums", bufs=4))
        turned = ctx.enter_context(tc.psum_pool(name="turned", bufs=4))
        ctx.enter_context(tc.manual_schedule())

        w1 = [keep.tile([P, INNER], U32, name="w1_%d" % g, align_bytes=256) for g in range(GROUPS * PASSES_1)]
        w2 = [keep.tile([P, HIDDEN], U32, name="w2_%d" % g, align_bytes=256) for g in range(GROUPS * PASSES_2)]
        b1_t = keep.tile([P, GROUPS * PASSES_2 + 4, PACK], F32, align_bytes=256)
        hf_rows = keep.tile([P, GROUPS, HIDDEN], BF16, align_bytes=64)
        w1_planes = [
            keep.tile([P, INNER], U8, name="w1_planes_%d" % s, align_bytes=64)
            for s in range(GROUPS * PASSES_1 // SHARED)
        ]
        w2_planes = [
            keep.tile([P, HIDDEN], U8, name="w2_planes_%d" % s, align_bytes=64)
            for s in range(GROUPS * PASSES_2 // SHARED)
        ]
        b1_rows = keep.tile([P, K_PASS], BF16)
        b2_rows = keep.tile([P, HIDDEN], BF16)
        ident_f32 = keep.tile([P, P], F32)
        ident_bf16 = keep.tile([P, P], BF16)

        nc.vector.memset(w1_planes[0][:].bitcast(I32), 0)
        nc.vector.memset(b1_rows[:], 0.0)
        nc.vector.memset(b2_rows[:], 0.0)
        nc.vector.memset(w1_planes[1][:].bitcast(I32), 0)
        for planes in w2_planes:
            nc.vector.memset(planes[:].bitcast(I32), 0)
        make_identity(nc, ident_f32[:])
        make_identity(nc, ident_bf16[:])

        nc.sync.dma_start(out=hf_rows[:], in_=hf.rearrange("(e p) k -> p e k", p=P))
        nc.scalar.dma_start(out=b1_rows[0 : GROUPS * PASSES_2, :], in_=g1_b.rearrange("e (j c) -> (e j) c", c=K_PASS))
        nc.scalar.dma_start(out=b2_rows[0:GROUPS, :], in_=g2_b)
        for s in range(len(w1_planes)):
            load_words(nc, w1[SHARED * s], g1_w_words[SHARED * s])
            load_planes(nc, w1_planes[s], g1_w_scales[SHARED * s : SHARED * (s + 1)])
            for g in range(SHARED * s + 1, SHARED * (s + 1)):
                load_words(nc, w1[g], g1_w_words[g])
        for s in range(len(w2_planes)):
            load_planes(nc, w2_planes[s], g2_w_scales[SHARED * s : SHARED * (s + 1)])
            for g in range(SHARED * s, SHARED * (s + 1)):
                load_words(nc, w2[g], g2_w_words[g])

        hf_grouped = keep.tile([P, GROUPS, PASSES_1 * P * 2], F32, align_bytes=64)
        hf_codes = keep.tile([P, GROUPS, PASSES_1 * P], U32, align_bytes=64)
        hf_scales = keep.tile([P, GROUPS, PASSES_1 * P], U8, align_bytes=64)
        for e in range(GROUPS):
            hf_words = hf_rows[:, e, :].bitcast(F32)
            hf_t = turned.tile([P, PASSES_1, 2, P], F32, tag="turned")
            for c in range(PASSES_1):
                for u in range(2):
                    nc.tensor.transpose(
                        out=hf_t[:, c, u, :],
                        in_=hf_words[:, 256 * c + u : 256 * (c + 1) : 2],
                        identity=ident_f32[:],
                    )
            nc.scalar.copy(
                out=hf_grouped[:, e, :].rearrange("p (c r u) -> p c r u", c=PASSES_1, u=2),
                in_=hf_t[:].rearrange("p c u r -> p c r u"),
            )
            nc.vector.quantize_mx(
                out=hf_codes[:, e, :].bitcast(FP8X4),
                scales=hf_scales[:, e, :],
                in_=hf_grouped[:, e, :].bitcast(BF16),
            )

        b2_all = keep.tile([P, GROUPS, HIDDEN], F32)
        for e in range(GROUPS):
            for h in range(HIDDEN // N_TILE):
                cols = slice(N_TILE * h, N_TILE * (h + 1))
                b2_sum = sums.tile([P, N_TILE], F32, tag="sum")
                nc.tensor.matmul(
                    out=b2_sum[:],
                    lhsT=ident_bf16[:, e : e + 1].to_broadcast([P, P]),
                    rhs=b2_rows[:, cols],
                    start=True,
                    stop=True,
                )
                if h == 0:
                    nc.scalar.copy(out=b2_all[:, e, cols], in_=b2_sum[:])
                else:
                    nc.vector.tensor_copy(out=b2_all[:, e, cols], in_=b2_sum[:])

        y_codes = [keep.tile([P, PASSES_2 * P], U32, name="y_codes_%d" % e, align_bytes=64) for e in range(GROUPS)]
        y_scales = [keep.tile([P, PASSES_2 * P], U8, name="y_scales_%d" % e, align_bytes=64) for e in range(GROUPS)]

        def multiply(unit):
            first_block = BLOCKS * unit
            y_rows = work.tile([P, BLOCKS, PACK, P], F32)
            for b in range(BLOCKS):
                e, j = divmod(first_block + b, PASSES_2)
                cols = slice(N_TILE * j, N_TILE * (j + 1))
                y_sum = sums.tile([P, N_TILE], F32, tag="sum")
                for c in range(PASSES_1):
                    g = PASSES_1 * e + c
                    nc.tensor.matmul_mx(
                        out=y_sum[:],
                        lhsT=hf_codes[:, e, P * c : P * (c + 1)].bitcast(FP8X4),
                        lhsT_scale=hf_scales[:, e, P * c : P * (c + 1)],
                        rhs=w1[g][:, cols].bitcast(FP8X4),
                        rhs_scale=w1_planes[g // SHARED][4 * (g % SHARED) : P, cols],
                        start=(c == 0),
                        stop=(c == PASSES_1 - 1),
                    )
                nc.scalar.copy(out=y_rows[:, b, :, :], in_=y_sum[:].rearrange("r (p t) -> r t p", t=PACK))
            return y_rows

        def turn_and_quantise(unit, y_rows):
            first_block = BLOCKS * unit
            y_grouped = work.tile([P, BLOCKS, P, PACK], BF16, align_bytes=64)
            for b in range(BLOCKS):
                y_t = turned.tile([P, PACK, P], F32, tag="turned")
                for t in range(PACK):
                    nc.tensor.transpose(out=y_t[:, t, :], in_=y_rows[:, b, t, :], identity=ident_f32[:])
                nc.vector.tensor_tensor(
                    out=y_grouped[:, b, :, :],
                    in0=y_t[:].rearrange("p t r -> p r t"),
                    in1=b1_t[:, first_block + b, :].unsqueeze(1).to_broadcast([P, P, PACK]),
                    op=ADD,
                )
            e, j = divmod(first_block, PASSES_2)
            nc.vector.quantize_mx(
                out=y_codes[e][:, P * j : P * (j + BLOCKS)].bitcast(FP8X4),
                scales=y_scales[e][:, P * j : P * (j + BLOCKS)],
                in_=y_grouped[:].rearrange("p b r t -> p (b r t)"),
            )

        waiting = multiply(0)

        b1_t_psum = turned.tile([P, PACK, P], BF16, tag="turned")
        for t in range(PACK):
            nc.tensor.transpose(out=b1_t_psum[:, t, :], in_=b1_rows[:, t:K_PASS:PACK], identity=ident_bf16[:])
        nc.vector.tensor_copy(
            out=b1_t[:, 0 : GROUPS * PASSES_2, :], in_=b1_t_psum[:, :, 0 : GROUPS * PASSES_2].rearrange("p t q -> p q t")
        )

        for unit in range(1, UNITS):
            fresh = multiply(unit)
            turn_and_quantise(unit - 1, waiting)
            waiting = fresh
        turn_and_quantise(UNITS - 1, waiting)

        for e in range(GROUPS):
            out_sums = [sums.tile([P, N_TILE], F32, name="out_sum_%d" % h, tag="sum") for h in range(HIDDEN // N_TILE)]
            for j in range(PASSES_2):
                g = PASSES_2 * e + j
                for h in range(HIDDEN // N_TILE):
                    cols = slice(N_TILE * h, N_TILE * (h + 1))
                    nc.tensor.matmul_mx(
                        out=out_sums[h][:],
                        lhsT=y_codes[e][:, P * j : P * (j + 1)].bitcast(FP8X4),
                        lhsT_scale=y_scales[e][:, P * j : P * (j + 1)],
                        rhs=w2[g][:, cols].bitcast(FP8X4),
                        rhs_scale=w2_planes[g // SHARED][4 * (g % SHARED) : P, cols],
                        start=(j == 0),
                        stop=(j == PASSES_2 - 1),
                    )
            for h in range(HIDDEN // N_TILE):
                cols = slice(N_TILE * h, N_TILE * (h + 1))
                result = results.tile([P, N_TILE], F32)
                nc.vector.tensor_tensor(out=result[:], in0=out_sums[h][:], in1=b2_all[:, e, cols], op=ADD)
                nc.sync.dma_start(out=out[P * e : P * (e + 1), cols], in_=result[:])
